import numpy as np
import ml_dtypes


def mxq(x, axis, fmt="e4m3"):
    dtype, down = {"e4m3": (ml_dtypes.float8_e4m3fn, 7), "e5m2": (ml_dtypes.float8_e5m2, 14)}[fmt]
    v = np.moveaxis(np.asarray(x, np.float32).astype(ml_dtypes.bfloat16).astype(np.float64), axis, -1)
    blocks = v.reshape(v.shape[:-1] + (-1, 32))
    amax = np.abs(blocks).max(-1, keepdims=True)
    byte = np.maximum(np.where(amax > 0, np.frexp(amax)[1] - 1 + 127, 0) - down, 1)
    scale = np.exp2(byte - 127.0)
    codes = (blocks / scale).astype(np.float32).astype(dtype).astype(np.float64)
    return np.moveaxis((codes * scale).reshape(v.shape), -1, axis)


WIDE = False


def mx_kscale(k):
    if not WIDE:
        return np.ones(k)
    levels = np.array([10, -10, 5, -5, 0])
    if k % 512:
        return np.exp2(np.random.permutation(np.resize(levels, k // 32))).repeat(32)
    a = np.empty((k // 512, 16))
    for p in range(k // 512):
        a[p, :8] = np.random.permutation(np.resize(levels, 8))
        for g in range(8):
            far = levels[np.abs(levels - a[p, g]) >= 10]
            a[p, g + 8] = far[np.random.randint(len(far))]
    return np.exp2(a.ravel()).repeat(32)


BF16 = ml_dtypes.bfloat16


def bf(x):
    return np.asarray(x, np.float32).astype(BF16)


def f64(x):
    return np.asarray(x).astype(np.float64)


B, IN, OUT = 512, 2048, 2048


def setup_inputs():
    s = mx_kscale(IN)
    return {"input_data": bf(np.random.standard_normal((B, IN)) * s),
            "weight": bf(np.random.standard_normal((OUT, IN)) / np.sqrt(IN) / s),
            "bias": bf(np.random.standard_normal(OUT) * 0.5),
            "prev_grad": bf(np.random.standard_normal((OUT, IN)) / np.sqrt(IN) / s),
            "prev_bias_grad": bf(np.random.standard_normal(OUT) * 0.5),
            "lr_samples": bf(np.random.uniform(0.1, 1.0, B))}


def reference(input_data, weight, bias, prev_grad, prev_bias_grad, lr_samples):
    xq = mxq(f64(input_data), 1, "e4m3")
    base = (xq @ mxq(f64(weight), 1, "e4m3").T) + f64(bias)
    pert = (xq @ mxq(f64(prev_grad), 1, "e4m3").T) + f64(prev_bias_grad)
    return base - f64(lr_samples)[:, None] * pert

@@ -1,0 +1,252 @@
+from contextlib import ExitStack
+
+import concourse.masks as masks
+import concourse.mybir as mybir
+
+F32 = mybir.dt.float32
+BF16 = mybir.dt.bfloat16
+U32 = mybir.dt.uint32
+U8 = mybir.dt.uint8
+FP8X4 = mybir.dt.float8_e4m3fn_x4
+ALU = mybir.AluOpType
+
+P = 128
+B = 512
+K = 2048
+O = 2048
+PASSES = K // 512
+NBT = B // P
+CHUNK = 512
+FLOPS = 2 * 2 * B * K * O
+
+RAW_BUFS = 5
+
+
+def tile_optimizedlinear_kernel(
+    tc, input_data, weight, bias, prev_grad, prev_bias_grad, lr_samples, out
+):
+    nc = tc.nc
+    with ExitStack() as ctx:
+        consts = ctx.enter_context(tc.tile_pool(name="consts", bufs=1))
+        rawp = ctx.enter_context(tc.tile_pool(name="rawp", bufs=RAW_BUFS))
+        grpp = ctx.enter_context(tc.tile_pool(name="grpp", bufs=2))
+        codp = ctx.enter_context(tc.tile_pool(name="codp", bufs=3))
+        cpool = ctx.enter_context(tc.tile_pool(name="cpool", bufs=2))
+        opool = ctx.enter_context(tc.tile_pool(name="opool", bufs=2))
+        psum = ctx.enter_context(tc.psum_pool(name="psum", bufs=8))
+        ctx.enter_context(tc.manual_schedule())
+
+        x_v = input_data.rearrange("(t p) k -> p t k", p=P)
+        w_v = weight.rearrange("(t p) k -> p t k", p=P)
+        g_v = prev_grad.rearrange("(t p) k -> p t k", p=P)
+
+        units = [("x", x_v, 0, 2), ("x", x_v, 2, 2)]
+        units += [("w", w_v, 0, 2), ("w", w_v, 2, 2), ("g", g_v, 0, 2), ("g", g_v, 2, 2)]
+        for ch in range(1, O // CHUNK):
+            units += [("w", w_v, 4 * ch, 4), ("g", g_v, 4 * ch, 4)]
+        n_units = len(units)
+
+        rows = consts.tile([P, CHUNK], BF16)
+        nc.gpsimd.memset(rows[:].bitcast(F32), 0.0)
+        ident_bf = consts.tile([P, P], BF16)
+        masks.make_identity(nc, ident_bf[:])
+        ident = consts.tile([P, P], F32)
+        masks.make_identity(nc, ident[:])
+        nc.sync.dma_start(out=rows[0:4, :], in_=bias.rearrange("(r n) -> r n", n=CHUNK))
+        nc.sync.dma_start(out=rows[4:8, :], in_=prev_bias_grad.rearrange("(r n) -> r n", n=CHUNK))
+        nc.sync.dma_start(out=rows[8:12, 0:P], in_=lr_samples.rearrange("(t p) -> t p", p=P))
+        neg_lr = consts.tile([P, NBT], F32)
+        bias_bc = consts.tile([P, O], F32)
+        pbias_bc = consts.tile([P, O], F32)
+
+        raws = {}
+
+        def load(i):
+            kind, view, t0, n = units[i]
+            raw = rawp.tile([P, 4, K], BF16, name="raw%d" % i, tag="raw")
+            nc.sync.dma_start(out=raw[:, 0:n, :], in_=view[:, t0 : t0 + n, :])
+            raws[i] = raw
+
+        grouped = {}
+        codes = {}
+        planes = {}
+
+        def transposes(i, pattern):
+            kind, view, t0, n = units[i]
+            width = n * P
+            raw_w = raws[i][:].bitcast(F32)
+            grp = grpp.tile([P, PASSES, 4 * width], BF16, name="grp%d" % i, tag="grp", align_bytes=64)
+            grouped[i] = grp
+            grp_w = grp[:].bitcast(F32)
+            b = 0
+            for g in range(PASSES):
+                for h in range(n // 2):
+                    bank = psum.tile([P, 512], F32, name="bank%d_%d" % (i, b), tag="ps")
+                    for j in range(2):
+                        for u in range(2):
+                            s = 2 * j + u
+                            c0 = 256 * g + u
+                            nc.tensor.transpose(
+                                bank[:, s * P : (s + 1) * P], raw_w[:, 2 * h + j, c0 : c0 + 255 : 2], ident[:]
+                            )
+                    dst = grp_w[:, g, 512 * h : 512 * h + 512].rearrange("p (j o u) -> p j o u", j=2, u=2)
+                    src = bank[:].rearrange("p (j u o) -> p j o u", j=2, u=2)
+                    if pattern[b % len(pattern)] == "S":
+                        nc.scalar.copy(out=dst, in_=src)
+                    else:
+                        nc.vector.tensor_copy(out=dst, in_=src)
+                    b += 1
+
+        def alloc_codes(i):
+            kind, view, t0, n = units[i]
+            width = n * P
+            if kind == "x":
+                cod = consts.tile([P, 48 + PASSES * width], U32, name="xcod%d" % i, align_bytes=256)
+                pla = consts.tile([P, PASSES, 2, 256], U8, name="xpla%d" % i, align_bytes=256)
+                codes[i] = cod[:, 48:].rearrange("p (g n) -> p g n", g=PASSES)
+                planes[i] = pla
+            else:
+                cod = codp.tile([P, PASSES, width], U32, name="cod%d" % i, tag="cod", align_bytes=256)
+                pla = codp.tile([P, PASSES, width], U8, name="pla%d" % i, tag="pla", align_bytes=256)
+                codes[i] = cod
+                planes[i] = pla
+
+        def quantise(i, g0):
+            if g0 == 0:
+                alloc_codes(i)
+            if units[i][0] == "x":
+                for g in (g0, g0 + 1):
+                    for j in range(2):
+                        nc.vector.quantize_mx(
+                            out=codes[i][:, g, j * P : (j + 1) * P].bitcast(FP8X4),
+                            scales=planes[i][:, g, j, 0:P],
+                            in_=grouped[i][:, g, j * 4 * P : (j + 1) * 4 * P],
+                        )
+                return
+            nc.vector.quantize_mx(
+                out=codes[i][:, g0 : g0 + 2, :].rearrange("p g n -> p (g n)").bitcast(FP8X4),
+                scales=planes[i][:, g0 : g0 + 2, :].rearrange("p g n -> p (g n)"),
+                in_=grouped[i][:, g0 : g0 + 2, :].rearrange("p g c -> p (g c)"),
+            )
+
+        c_tiles = {}
+        o_tiles = {}
+
+        def c_job(ch, bt):
+            if ch not in c_tiles:
+                c_tiles[ch] = cpool.tile([P, NBT, CHUNK], F32, name="c%d" % ch, tag="c")
+            cols = slice(ch * CHUNK, (ch + 1) * CHUNK)
+            nc.vector.scalar_tensor_tensor(
+                out=c_tiles[ch][:, bt, :],
+                in0=pbias_bc[:, cols],
+                scalar=neg_lr[:, bt : bt + 1],
+                in1=bias_bc[:, cols],
+                op0=ALU.mult,
+                op1=ALU.add,
+            )
+
+        def mx_group(i, bt, first=0, width=None):
+            kind, view, t0, n = units[i]
+            if width is None:
+                width = n * P
+            acc = psum.tile([P, 512], F32, name="acc%d_%d_%d" % (i, bt, first), tag="ps")
+            xi = bt // 2
+            xs = slice((bt % 2) * P, (bt % 2) * P + P)
+            for g in range(PASSES):
+                nc.tensor.matmul_mx(
+                    out=acc[:, 0:width],
+                    lhsT=codes[xi][:, g, xs].bitcast(FP8X4),
+                    lhsT_scale=planes[xi][:, g, bt % 2, 0:P],
+                    rhs=codes[i][:, g, first : first + width].bitcast(FP8X4),
+                    rhs_scale=planes[i][:, g, first : first + width],
+                    start=(g == 0),
+                    stop=(g == PASSES - 1),
+                )
+            ch = (t0 * P) // CHUNK
+            lo = t0 * P - ch * CHUNK + first
+            if ch not in o_tiles:
+                o_tiles[ch] = opool.tile([P, NBT, CHUNK], F32, name="o%d" % ch, tag="o")
+            o_sl = o_tiles[ch][:, bt, lo : lo + width]
+            if kind == "w":
+                nc.vector.tensor_tensor(
+                    out=o_sl, in0=acc[:, 0:width], in1=c_tiles[ch][:, bt, lo : lo + width], op=ALU.add
+                )
+            else:
+                nc.vector.scalar_tensor_tensor(
+                    out=o_sl,
+                    in0=acc[:, 0:width],
+                    scalar=neg_lr[:, bt : bt + 1],
+                    in1=o_sl,
+                    op0=ALU.mult,
+                    op1=ALU.add,
+                )
+                nc.sync.dma_start(
+                    out=out[bt * P : (bt + 1) * P, ch * CHUNK + lo : ch * CHUNK + lo + width], in_=o_sl
+                )
+
+        for i in range(RAW_BUFS):
+            load(i)
+
+        def next_load(i):
+            if i + RAW_BUFS < n_units:
+                load(i + RAW_BUFS)
+
+        lr_ps = psum.tile([P, 512], F32, name="lr_ps", tag="ps")
+        nc.tensor.matmul(out=lr_ps[:, 0:32], lhsT=rows[:, 0:P], rhs=ident_bf[:, 0:32], start=True, stop=True)
+        nc.vector.tensor_scalar_mul(out=neg_lr[:], in0=lr_ps[:, 8:12], scalar1=-1.0)
+
+        def spread(ch):
+            for r, dst_t, eng in ((ch, bias_bc, "S"), (4 + ch, pbias_bc, "V" if ch == 0 else "S")):
+                bc = psum.tile([P, 512], F32, name="bc%d" % r, tag="ps")
+                nc.tensor.matmul(
+                    out=bc[:], lhsT=ident_bf[:, r : r + 1].to_broadcast([P, P]), rhs=rows[:], start=True, stop=True
+                )
+                dst = dst_t[:, ch * CHUNK : (ch + 1) * CHUNK]
+                if eng == "S":
+                    nc.scalar.copy(out=dst, in_=bc[:])
+                else:
+                    nc.vector.tensor_copy(out=dst, in_=bc[:])
+
+        spread(0)
+        for bt in range(NBT):
+            c_job(0, bt)
+        for i in range(3):
+            transposes(i, "SV")
+            next_load(i)
+            quantise(i, 0)
+            quantise(i, 2)
+            spread(i + 1)
+
+        extra = {}
+        for i in range(2, n_units):
+            kind, view, t0, n = units[i]
+            ch = (t0 * P) // CHUNK
+            if ch + 1 >= O // CHUNK:
+                extra[i] = []
+            elif n == 2:
+                extra[i] = [(ch + 1, (0 if kind == "w" else 2) + (t0 % 4) // 2)]
+            else:
+                extra[i] = [(ch + 1, 0), (ch + 1, 1)] if kind == "w" else [(ch + 1, 2), (ch + 1, 3)]
+
+        for i in range(2, n_units):
+            nxt = i + 1
+            if nxt < n_units:
+                transposes(nxt, "S")
+                next_load(nxt)
+                quantise(nxt, 0)
+            jobs = extra[i]
+            if nxt == n_units:
+                for bt in range(NBT):
+                    mx_group(i, bt, 0, 256)
+                    mx_group(i, bt, 256, 256)
+                break
+            mx_group(i, 0)
+            if len(jobs) > 0:
+                c_job(jobs[0][0], jobs[0][1])
+            mx_group(i, 1)
+            if nxt < n_units:
+                quantise(nxt, 2)
+            mx_group(i, 2)
+            if len(jobs) > 1:
+                c_job(jobs[1][0], jobs[1][1])
+            mx_group(i, 3)

@@ -19,7 +19,7 @@ NBT = B // P
 CHUNK = 512
 FLOPS = 2 * 2 * B * K * O
 
-RAW_BUFS = 5
+RAW_BUFS = 8
 
 
 def tile_optimizedlinear_kernel(
@@ -29,9 +29,9 @@ def tile_optimizedlinear_kernel(
     with ExitStack() as ctx:
         consts = ctx.enter_context(tc.tile_pool(name="consts", bufs=1))
         rawp = ctx.enter_context(tc.tile_pool(name="rawp", bufs=RAW_BUFS))
+        ordp = ctx.enter_context(tc.tile_pool(name="ordp", bufs=2))
         grpp = ctx.enter_context(tc.tile_pool(name="grpp", bufs=2))
         codp = ctx.enter_context(tc.tile_pool(name="codp", bufs=3))
-        cpool = ctx.enter_context(tc.tile_pool(name="cpool", bufs=2))
         opool = ctx.enter_context(tc.tile_pool(name="opool", bufs=2))
         psum = ctx.enter_context(tc.psum_pool(name="psum", bufs=8))
         ctx.enter_context(tc.manual_schedule())
@@ -46,38 +46,119 @@ def tile_optimizedlinear_kernel(
             units += [("w", w_v, 4 * ch, 4), ("g", g_v, 4 * ch, 4)]
         n_units = len(units)
 
-        rows = consts.tile([P, CHUNK], BF16)
-        nc.gpsimd.memset(rows[:].bitcast(F32), 0.0)
-        ident_bf = consts.tile([P, P], BF16)
-        masks.make_identity(nc, ident_bf[:])
+        raws = {}
+        pending = []
+        for i in range(n_units):
+            for h in range(units[i][3] // 2):
+                pending.append((i, h))
+
+        def load_next():
+            if len(pending) == 0:
+                return
+            i, h = pending[0]
+            pending.remove((i, h))
+            kind, view, t0, n = units[i]
+            raw = rawp.tile([P, 2, K], BF16, name="raw%d_%d" % (i, h), tag="raw")
+            if i < 4:
+                for j in range(2):
+                    nc.sync.dma_start(out=raw[:, j, :], in_=view[:, t0 + 2 * h + j, :])
+            else:
+                nc.sync.dma_start(out=raw[:], in_=view[:, t0 + 2 * h : t0 + 2 * h + 2, :])
+            raws[(i, h)] = raw
+
+        load_next()
+        load_next()
+
         ident = consts.tile([P, P], F32)
         masks.make_identity(nc, ident[:])
-        nc.sync.dma_start(out=rows[0:4, :], in_=bias.rearrange("(r n) -> r n", n=CHUNK))
-        nc.sync.dma_start(out=rows[4:8, :], in_=prev_bias_grad.rearrange("(r n) -> r n", n=CHUNK))
-        nc.sync.dma_start(out=rows[8:12, 0:P], in_=lr_samples.rearrange("(t p) -> t p", p=P))
+        left = consts.tile([P, B], BF16)
+        nc.gpsimd.memset(left[:].bitcast(F32), 0.0)
+        nc.gpsimd.memset(left[0:1, :], -1.0)
+        right = consts.tile([P, O], BF16)
+        nc.vector.memset(right[:].bitcast(F32), 0.0)
+        ident_bf = consts.tile([P, P], BF16)
+        masks.make_identity(nc, ident_bf[:])
+        nc.sync.dma_start(out=left[1:2, :], in_=lr_samples.rearrange("(r n) -> r n", n=B))
+        nc.sync.dma_start(out=right[0:1, :], in_=bias.rearrange("(r n) -> r n", n=O))
+        nc.sync.dma_start(out=right[1:2, :], in_=prev_bias_grad.rearrange("(r n) -> r n", n=O))
+        for i in range(2, RAW_BUFS):
+            load_next()
         neg_lr = consts.tile([P, NBT], F32)
-        bias_bc = consts.tile([P, O], F32)
-        pbias_bc = consts.tile([P, O], F32)
+        d_all = consts.tile([P, NBT, O], F32)
 
-        raws = {}
+        def copy(eng, dst, src):
+            if eng == "S":
+                nc.scalar.copy(out=dst, in_=src)
+            else:
+                nc.vector.tensor_copy(out=dst, in_=src)
 
-        def load(i):
-            kind, view, t0, n = units[i]
-            raw = rawp.tile([P, 4, K], BF16, name="raw%d" % i, tag="raw")
-            nc.sync.dma_start(out=raw[:, 0:n, :], in_=view[:, t0 : t0 + n, :])
-            raws[i] = raw
+        def d_job(ch, bt, eng):
+            bank = psum.tile([P, 512], F32, name="d%d_%d" % (ch, bt), tag="ps")
+            cols = slice(ch * CHUNK, (ch + 1) * CHUNK)
+            nc.tensor.matmul(
+                out=bank[:], lhsT=left[:, bt * P : (bt + 1) * P], rhs=right[:, cols], start=True, stop=True
+            )
+            copy(eng, d_all[:, bt, cols], bank[:])
 
         grouped = {}
         codes = {}
         planes = {}
+        ordered = {}
+
+        def reorder(i, j, eng):
+            if i not in ordered:
+                ordered[i] = ordp.tile([P, 4, K // 2], F32, name="ord%d" % i, tag="ord")
+            src = raws[(i, j // 2)][:].bitcast(F32)[:, j % 2, :].rearrange("p (m u) -> p u m", u=2)
+            dst = ordered[i][:, j, :].rearrange("p (u m) -> p u m", u=2)
+            copy(eng, dst, src)
+            if j % 2 == 1:
+                load_next()
+
+        def words(i, j, g, u):
+            if i in ordered:
+                c0 = 512 * u + P * g
+                return ordered[i][:, j, c0 : c0 + P]
+            c0 = 256 * g + u
+            return raws[(i, j // 2)][:].bitcast(F32)[:, j % 2, c0 : c0 + 255 : 2]
+
+        def row_tile_transposes(i, j, grp_w, engines):
+            for half in range(2):
+                bank = psum.tile([P, 512], F32, name="bank%d_%d_%d" % (i, j, half), tag="ps")
+                for gi in range(2):
+                    for u in range(2):
+                        s = 2 * gi + u
+                        nc.tensor.transpose(bank[:, s * P : (s + 1) * P], words(i, j, 2 * half + gi, u), ident[:])
+                copy(
+                    engines[half],
+                    grp_w[:, 2 * half : 2 * half + 2, :].rearrange("p g (o u) -> p g o u", u=2),
+                    bank[:].rearrange("p (g u o) -> p g o u", g=2, u=2),
+                )
+
+        def x_tile(t):
+            i, j = t // 2, t % 2
+            grp = grpp.tile([P, PASSES, 4 * P], BF16, name="xgrp%d" % t, tag="xgrp", align_bytes=64)
+            row_tile_transposes(i, j, grp[:].bitcast(F32), "SV")
+            cod = consts.tile([P, PASSES, P], U32, name="xcod%d" % t, align_bytes=256)
+            pla = consts.tile([P, PASSES, P], U8, name="xpla%d" % t, align_bytes=256)
+            codes[("x", t)] = cod
+            planes[("x", t)] = pla
+            grouped[("x", t)] = grp
+
+        def x_quantise(t):
+            nc.vector.quantize_mx(
+                out=codes[("x", t)][:].rearrange("p g n -> p (g n)").bitcast(FP8X4),
+                scales=planes[("x", t)][:].rearrange("p g n -> p (g n)"),
+                in_=grouped[("x", t)][:].rearrange("p g c -> p (g c)"),
+            )
+
+        def make_grouped(i):
+            width = units[i][3] * P
+            grouped[i] = grpp.tile([P, PASSES, 4 * width], BF16, name="grp%d" % i, tag="grp", align_bytes=64)
 
         def transposes(i, pattern):
-            kind, view, t0, n = units[i]
-            width = n * P
-            raw_w = raws[i][:].bitcast(F32)
-            grp = grpp.tile([P, PASSES, 4 * width], BF16, name="grp%d" % i, tag="grp", align_bytes=64)
-            grouped[i] = grp
-            grp_w = grp[:].bitcast(F32)
+            n = units[i][3]
+            make_grouped(i)
+            grp_w = grouped[i][:].bitcast(F32)
             b = 0
             for g in range(PASSES):
                 for h in range(n // 2):
@@ -85,91 +166,53 @@ def tile_optimizedlinear_kernel(
                     for j in range(2):
                         for u in range(2):
                             s = 2 * j + u
-                            c0 = 256 * g + u
                             nc.tensor.transpose(
-                                bank[:, s * P : (s + 1) * P], raw_w[:, 2 * h + j, c0 : c0 + 255 : 2], ident[:]
+                                bank[:, s * P : (s + 1) * P], words(i, 2 * h + j, g, u), ident[:]
                             )
-                    dst = grp_w[:, g, 512 * h : 512 * h + 512].rearrange("p (j o u) -> p j o u", j=2, u=2)
-                    src = bank[:].rearrange("p (j u o) -> p j o u", j=2, u=2)
-                    if pattern[b % len(pattern)] == "S":
-                        nc.scalar.copy(out=dst, in_=src)
-                    else:
-                        nc.vector.tensor_copy(out=dst, in_=src)
+                    copy(
+                        pattern[b % len(pattern)],
+                        grp_w[:, g, 512 * h : 512 * h + 512].rearrange("p (j o u) -> p j o u", j=2, u=2),
+                        bank[:].rearrange("p (j u o) -> p j o u", j=2, u=2),
+                    )
                     b += 1
 
-        def alloc_codes(i):
-            kind, view, t0, n = units[i]
-            width = n * P
-            if kind == "x":
-                cod = consts.tile([P, 48 + PASSES * width], U32, name="xcod%d" % i, align_bytes=256)
-                pla = consts.tile([P, PASSES, 2, 256], U8, name="xpla%d" % i, align_bytes=256)
-                codes[i] = cod[:, 48:].rearrange("p (g n) -> p g n", g=PASSES)
-                planes[i] = pla
-            else:
-                cod = codp.tile([P, PASSES, width], U32, name="cod%d" % i, tag="cod", align_bytes=256)
-                pla = codp.tile([P, PASSES, width], U8, name="pla%d" % i, tag="pla", align_bytes=256)
-                codes[i] = cod
-                planes[i] = pla
-
         def quantise(i, g0):
+            width = units[i][3] * P
             if g0 == 0:
-                alloc_codes(i)
-            if units[i][0] == "x":
-                for g in (g0, g0 + 1):
-                    for j in range(2):
-                        nc.vector.quantize_mx(
-                            out=codes[i][:, g, j * P : (j + 1) * P].bitcast(FP8X4),
-                            scales=planes[i][:, g, j, 0:P],
-                            in_=grouped[i][:, g, j * 4 * P : (j + 1) * 4 * P],
-                        )
-                return
+                codes[i] = codp.tile([P, PASSES, width], U32, name="cod%d" % i, tag="cod", align_bytes=256)
+                planes[i] = codp.tile([P, PASSES, width], U8, name="pla%d" % i, tag="pla", align_bytes=256)
             nc.vector.quantize_mx(
                 out=codes[i][:, g0 : g0 + 2, :].rearrange("p g n -> p (g n)").bitcast(FP8X4),
                 scales=planes[i][:, g0 : g0 + 2, :].rearrange("p g n -> p (g n)"),
                 in_=grouped[i][:, g0 : g0 + 2, :].rearrange("p g c -> p (g c)"),
             )
 
-        c_tiles = {}
         o_tiles = {}
-
-        def c_job(ch, bt):
-            if ch not in c_tiles:
-                c_tiles[ch] = cpool.tile([P, NBT, CHUNK], F32, name="c%d" % ch, tag="c")
-            cols = slice(ch * CHUNK, (ch + 1) * CHUNK)
-            nc.vector.scalar_tensor_tensor(
-                out=c_tiles[ch][:, bt, :],
-                in0=pbias_bc[:, cols],
-                scalar=neg_lr[:, bt : bt + 1],
-                in1=bias_bc[:, cols],
-                op0=ALU.mult,
-                op1=ALU.add,
-            )
 
         def mx_group(i, bt, first=0, width=None):
             kind, view, t0, n = units[i]
             if width is None:
                 width = n * P
             acc = psum.tile([P, 512], F32, name="acc%d_%d_%d" % (i, bt, first), tag="ps")
-            xi = bt // 2
-            xs = slice((bt % 2) * P, (bt % 2) * P + P)
             for g in range(PASSES):
                 nc.tensor.matmul_mx(
                     out=acc[:, 0:width],
-                    lhsT=codes[xi][:, g, xs].bitcast(FP8X4),
-                    lhsT_scale=planes[xi][:, g, bt % 2, 0:P],
+                    lhsT=codes[("x", bt)][:, g, :].bitcast(FP8X4),
+                    lhsT_scale=planes[("x", bt)][:, g, :],
                     rhs=codes[i][:, g, first : first + width].bitcast(FP8X4),
                     rhs_scale=planes[i][:, g, first : first + width],
                     start=(g == 0),
                     stop=(g == PASSES - 1),
                 )
             ch = (t0 * P) // CHUNK
-            lo = t0 * P - ch * CHUNK + first
+            col = t0 * P + first
+            lo = col - ch * CHUNK
             if ch not in o_tiles:
                 o_tiles[ch] = opool.tile([P, NBT, CHUNK], F32, name="o%d" % ch, tag="o")
             o_sl = o_tiles[ch][:, bt, lo : lo + width]
             if kind == "w":
                 nc.vector.tensor_tensor(
-                    out=o_sl, in0=acc[:, 0:width], in1=c_tiles[ch][:, bt, lo : lo + width], op=ALU.add
+                    out=o_sl, in0=acc[:, 0:width], in1=d_all[:, bt, col : col + width], op=ALU.subtract
                 )
             else:
                 nc.vector.scalar_tensor_tensor(
@@ -180,42 +223,46 @@ def tile_optimizedlinear_kernel(
                     op0=ALU.mult,
                     op1=ALU.add,
                 )
-                nc.sync.dma_start(
-                    out=out[bt * P : (bt + 1) * P, ch * CHUNK + lo : ch * CHUNK + lo + width], in_=o_sl
-                )
+                nc.sync.dma_start(out=out[bt * P : (bt + 1) * P, col : col + width], in_=o_sl)
 
-        for i in range(RAW_BUFS):
-            load(i)
-
-        def next_load(i):
-            if i + RAW_BUFS < n_units:
-                load(i + RAW_BUFS)
+        x_tile(0)
+        x_tile(1)
+        x_quantise(0)
+        x_tile(2)
+        x_quantise(1)
+        load_next()
+        x_tile(3)
+        x_quantise(2)
+        load_next()
 
         lr_ps = psum.tile([P, 512], F32, name="lr_ps", tag="ps")
-        nc.tensor.matmul(out=lr_ps[:, 0:32], lhsT=rows[:, 0:P], rhs=ident_bf[:, 0:32], start=True, stop=True)
-        nc.vector.tensor_scalar_mul(out=neg_lr[:], in0=lr_ps[:, 8:12], scalar1=-1.0)
-
-        def spread(ch):
-            for r, dst_t, eng in ((ch, bias_bc, "S"), (4 + ch, pbias_bc, "V" if ch == 0 else "S")):
-                bc = psum.tile([P, 512], F32, name="bc%d" % r, tag="ps")
-                nc.tensor.matmul(
-                    out=bc[:], lhsT=ident_bf[:, r : r + 1].to_broadcast([P, P]), rhs=rows[:], start=True, stop=True
-                )
-                dst = dst_t[:, ch * CHUNK : (ch + 1) * CHUNK]
-                if eng == "S":
-                    nc.scalar.copy(out=dst, in_=bc[:])
-                else:
-                    nc.vector.tensor_copy(out=dst, in_=bc[:])
-
-        spread(0)
         for bt in range(NBT):
-            c_job(0, bt)
-        for i in range(3):
-            transposes(i, "SV")
-            next_load(i)
-            quantise(i, 0)
-            quantise(i, 2)
-            spread(i + 1)
+            nc.tensor.matmul(
+                out=lr_ps[:, bt : bt + 1],
+                lhsT=left[:, bt * P : (bt + 1) * P],
+                rhs=ident_bf[:, 1:2],
+                start=True,
+                stop=True,
+            )
+        d_job(0, 0, "S")
+        d_job(0, 1, "S")
+
+        make_grouped(2)
+        grp_w = grouped[2][:].bitcast(F32)
+        row_tile_transposes(2, 0, grp_w[:, :, 0:256], "SV")
+        nc.vector.tensor_scalar_mul(out=neg_lr[:], in0=lr_ps[:, 0:NBT], scalar1=-1.0)
+        x_quantise(3)
+        row_tile_transposes(2, 1, grp_w[:, :, 256:512], "SV")
+        load_next()
+        quantise(2, 0)
+        quantise(2, 2)
+        make_grouped(3)
+        grp_w = grouped[3][:].bitcast(F32)
+        row_tile_transposes(3, 0, grp_w[:, :, 0:256], "SS")
+        d_job(0, 2, "S")
+        d_job(0, 3, "S")
+        row_tile_transposes(3, 1, grp_w[:, :, 256:512], "SS")
+        load_next()
 
         extra = {}
         for i in range(2, n_units):
@@ -230,23 +277,31 @@ def tile_optimizedlinear_kernel(
 
         for i in range(2, n_units):
             nxt = i + 1
+            far = i + 2
+            n_far = units[far][3] if far < n_units else 0
+            if n_far > 0:
+                reorder(far, 0, "V")
+            if n_far > 2:
+                reorder(far, 1, "V")
             if nxt < n_units:
-                transposes(nxt, "S")
-                next_load(nxt)
+                if nxt > 3:
+                    transposes(nxt, "S")
                 quantise(nxt, 0)
-            jobs = extra[i]
+            for ch, bt in extra[i]:
+                d_job(ch, bt, "S")
             if nxt == n_units:
                 for bt in range(NBT):
                     mx_group(i, bt, 0, 256)
                     mx_group(i, bt, 256, 256)
                 break
             mx_group(i, 0)
-            if len(jobs) > 0:
-                c_job(jobs[0][0], jobs[0][1])
+            if n_far == 2:
+                reorder(far, 1, "S")
             mx_group(i, 1)
-            if nxt < n_units:
-                quantise(nxt, 2)
+            quantise(nxt, 2)
+            if n_far > 2:
+                reorder(far, 2, "V")
             mx_group(i, 2)
-            if len(jobs) > 1:
-                c_job(jobs[1][0], jobs[1][1])
+            if n_far > 2:
+                reorder(far, 3, "S")
             mx_group(i, 3)

@@ -283,6 +283,9 @@ def tile_optimizedlinear_kernel(
                 reorder(far, 0, "V")
             if n_far > 2:
                 reorder(far, 1, "V")
+                reorder(far, 2, "V")
+                if i < 6:
+                    reorder(far, 3, "V")
             if nxt < n_units:
                 if nxt > 3:
                     transposes(nxt, "S")
@@ -296,12 +299,10 @@ def tile_optimizedlinear_kernel(
                 break
             mx_group(i, 0)
             if n_far == 2:
-                reorder(far, 1, "S")
+                reorder(far, 1, "V")
             mx_group(i, 1)
             quantise(nxt, 2)
-            if n_far > 2:
-                reorder(far, 2, "V")
             mx_group(i, 2)
-            if n_far > 2:
+            if n_far > 2 and i >= 6:
                 reorder(far, 3, "S")
             mx_group(i, 3)

@@ -41,7 +41,7 @@ def tile_optimizedlinear_kernel(
         g_v = prev_grad.rearrange("(t p) k -> p t k", p=P)
 
         units = [("x", x_v, 0, 2), ("x", x_v, 2, 2)]
-        units += [("w", w_v, 0, 2), ("w", w_v, 2, 2), ("g", g_v, 0, 2), ("g", g_v, 2, 2)]
+        units += [("w", w_v, 0, 2), ("w", w_v, 2, 2), ("g", g_v, 0, 4)]
         for ch in range(1, O // CHUNK):
             units += [("w", w_v, 4 * ch, 4), ("g", g_v, 4 * ch, 4)]
         n_units = len(units)
@@ -105,14 +105,13 @@ def tile_optimizedlinear_kernel(
         planes = {}
         ordered = {}
 
-        def reorder(i, j, eng):
+        def reorder(i, h, eng):
             if i not in ordered:
                 ordered[i] = ordp.tile([P, 4, K // 2], F32, name="ord%d" % i, tag="ord")
-            src = raws[(i, j // 2)][:].bitcast(F32)[:, j % 2, :].rearrange("p (m u) -> p u m", u=2)
-            dst = ordered[i][:, j, :].rearrange("p (u m) -> p u m", u=2)
+            src = raws[(i, h)][:].bitcast(F32).rearrange("p j (m u) -> p j u m", u=2)
+            dst = ordered[i][:, 2 * h : 2 * h + 2, :].rearrange("p j (u m) -> p j u m", u=2)
             copy(eng, dst, src)
-            if j % 2 == 1:
-                load_next()
+            load_next()
 
         def words(i, j, g, u):
             if i in ordered:
@@ -271,7 +270,7 @@ def tile_optimizedlinear_kernel(
             if ch + 1 >= O // CHUNK:
                 extra[i] = []
             elif n == 2:
-                extra[i] = [(ch + 1, (0 if kind == "w" else 2) + (t0 % 4) // 2)]
+                extra[i] = [(ch + 1, t0 // 2)]
             else:
                 extra[i] = [(ch + 1, 0), (ch + 1, 1)] if kind == "w" else [(ch + 1, 2), (ch + 1, 3)]
 
@@ -279,13 +278,8 @@ def tile_optimizedlinear_kernel(
             nxt = i + 1
             far = i + 2
             n_far = units[far][3] if far < n_units else 0
-            if n_far > 0:
-                reorder(far, 0, "V")
-            if n_far > 2:
-                reorder(far, 1, "V")
-                reorder(far, 2, "V")
-                if i < 6:
-                    reorder(far, 3, "V")
+            for h in range(n_far // 2):
+                reorder(far, h, "V")
             if nxt < n_units:
                 if nxt > 3:
                     transposes(nxt, "S")
@@ -298,11 +292,7 @@ def tile_optimizedlinear_kernel(
                     mx_group(i, bt, 256, 256)
                 break
             mx_group(i, 0)
-            if n_far == 2:
-                reorder(far, 1, "V")
             mx_group(i, 1)
             quantise(nxt, 2)
             mx_group(i, 2)
-            if n_far > 2 and i >= 6:
-                reorder(far, 3, "S")
             mx_group(i, 3)

@@ -29,9 +29,10 @@ def tile_optimizedlinear_kernel(
     with ExitStack() as ctx:
         consts = ctx.enter_context(tc.tile_pool(name="consts", bufs=1))
         rawp = ctx.enter_context(tc.tile_pool(name="rawp", bufs=RAW_BUFS))
-        ordp = ctx.enter_context(tc.tile_pool(name="ordp", bufs=2))
+        ordp = ctx.enter_context(tc.tile_pool(name="ordp", bufs=3))
         grpp = ctx.enter_context(tc.tile_pool(name="grpp", bufs=2))
         codp = ctx.enter_context(tc.tile_pool(name="codp", bufs=3))
+        dpool = ctx.enter_context(tc.tile_pool(name="dpool", bufs=2))
         opool = ctx.enter_context(tc.tile_pool(name="opool", bufs=2))
         psum = ctx.enter_context(tc.psum_pool(name="psum", bufs=8))
         ctx.enter_context(tc.manual_schedule())
@@ -84,7 +85,7 @@ def tile_optimizedlinear_kernel(
         for i in range(2, RAW_BUFS):
             load_next()
         neg_lr = consts.tile([P, NBT], F32)
-        d_all = consts.tile([P, NBT, O], F32)
+        d_tiles = {}
 
         def copy(eng, dst, src):
             if eng == "S":
@@ -98,20 +99,24 @@ def tile_optimizedlinear_kernel(
             nc.tensor.matmul(
                 out=bank[:], lhsT=left[:, bt * P : (bt + 1) * P], rhs=right[:, cols], start=True, stop=True
             )
-            copy(eng, d_all[:, bt, cols], bank[:])
+            if ch not in d_tiles:
+                d_tiles[ch] = dpool.tile([P, NBT, CHUNK], F32, name="dt%d" % ch, tag="d")
+            copy(eng, d_tiles[ch][:, bt, :], bank[:])
 
         grouped = {}
         codes = {}
         planes = {}
         ordered = {}
 
-        def reorder(i, h, eng):
+        def reorder(i, j0, j1, eng):
             if i not in ordered:
                 ordered[i] = ordp.tile([P, 4, K // 2], F32, name="ord%d" % i, tag="ord")
-            src = raws[(i, h)][:].bitcast(F32).rearrange("p j (m u) -> p j u m", u=2)
-            dst = ordered[i][:, 2 * h : 2 * h + 2, :].rearrange("p j (u m) -> p j u m", u=2)
+            n = j1 - j0
+            src = raws[(i, j0 // 2)][:, j0 % 2 : j0 % 2 + n, :].bitcast(F32).rearrange("p j (m u) -> p j u m", u=2)
+            dst = ordered[i][:, j0:j1, :].rearrange("p j (u m) -> p j u m", u=2)
             copy(eng, dst, src)
-            load_next()
+            if j1 % 2 == 0:
+                load_next()
 
         def words(i, j, g, u):
             if i in ordered:
@@ -136,7 +141,7 @@ def tile_optimizedlinear_kernel(
         def x_tile(t):
             i, j = t // 2, t % 2
             grp = grpp.tile([P, PASSES, 4 * P], BF16, name="xgrp%d" % t, tag="xgrp", align_bytes=64)
-            row_tile_transposes(i, j, grp[:].bitcast(F32), "SV")
+            row_tile_transposes(i, j, grp[:].bitcast(F32), "SS")
             cod = consts.tile([P, PASSES, P], U32, name="xcod%d" % t, align_bytes=256)
             pla = consts.tile([P, PASSES, P], U8, name="xpla%d" % t, align_bytes=256)
             codes[("x", t)] = cod
@@ -211,7 +216,7 @@ def tile_optimizedlinear_kernel(
             o_sl = o_tiles[ch][:, bt, lo : lo + width]
             if kind == "w":
                 nc.vector.tensor_tensor(
-                    out=o_sl, in0=acc[:, 0:width], in1=d_all[:, bt, col : col + width], op=ALU.subtract
+                    out=o_sl, in0=acc[:, 0:width], in1=d_tiles[ch][:, bt, lo : lo + width], op=ALU.subtract
                 )
             else:
                 nc.vector.scalar_tensor_tensor(
@@ -246,22 +251,22 @@ def tile_optimizedlinear_kernel(
         d_job(0, 0, "S")
         d_job(0, 1, "S")
 
-        make_grouped(2)
-        grp_w = grouped[2][:].bitcast(F32)
-        row_tile_transposes(2, 0, grp_w[:, :, 0:256], "SV")
+        def w_tile(i, j, engines):
+            if j == 0:
+                make_grouped(i)
+            reorder(i, j, j + 1, "V")
+            row_tile_transposes(i, j, grouped[i][:].bitcast(F32)[:, :, 256 * j : 256 * j + 256], engines)
+
+        w_tile(2, 0, "SS")
         nc.vector.tensor_scalar_mul(out=neg_lr[:], in0=lr_ps[:, 0:NBT], scalar1=-1.0)
         x_quantise(3)
-        row_tile_transposes(2, 1, grp_w[:, :, 256:512], "SV")
-        load_next()
+        w_tile(2, 1, "SS")
+        w_tile(3, 0, "SS")
+        w_tile(3, 1, "SS")
         quantise(2, 0)
         quantise(2, 2)
-        make_grouped(3)
-        grp_w = grouped[3][:].bitcast(F32)
-        row_tile_transposes(3, 0, grp_w[:, :, 0:256], "SS")
         d_job(0, 2, "S")
         d_job(0, 3, "S")
-        row_tile_transposes(3, 1, grp_w[:, :, 256:512], "SS")
-        load_next()
 
         extra = {}
         for i in range(2, n_units):
@@ -278,8 +283,12 @@ def tile_optimizedlinear_kernel(
             nxt = i + 1
             far = i + 2
             n_far = units[far][3] if far < n_units else 0
-            for h in range(n_far // 2):
-                reorder(far, h, "V")
+            if n_far > 0:
+                if far < 6:
+                    reorder(far, 0, 2, "V")
+                else:
+                    reorder(far, 1, 2, "V")
+                reorder(far, 2, 4, "V")
             if nxt < n_units:
                 if nxt > 3:
                     transposes(nxt, "S")
@@ -295,4 +304,6 @@ def tile_optimizedlinear_kernel(
             mx_group(i, 1)
             quantise(nxt, 2)
             mx_group(i, 2)
+            if i + 3 >= 6 and i + 3 < n_units:
+                reorder(i + 3, 0, 1, "S")
             mx_group(i, 3)

@@ -20,6 +20,10 @@ CHUNK = 512
 FLOPS = 2 * 2 * B * K * O
 
 RAW_BUFS = 8
+ND = 2
+SPREAD_BEFORE = (9, 0)
+
+REORDER = {4: "VV", 5: "VV", 6: "SVVV", 7: "TTVV", 8: "SVVV", 9: "SSVV", 10: "SSVV", 11: "SSVV"}
 
 
 def tile_optimizedlinear_kernel(
@@ -31,7 +35,7 @@ def tile_optimizedlinear_kernel(
         rawp = ctx.enter_context(tc.tile_pool(name="rawp", bufs=RAW_BUFS))
         ordp = ctx.enter_context(tc.tile_pool(name="ordp", bufs=3))
         grpp = ctx.enter_context(tc.tile_pool(name="grpp", bufs=2))
-        codp = ctx.enter_context(tc.tile_pool(name="codp", bufs=3))
+        codp = ctx.enter_context(tc.tile_pool(name="codp", bufs=2))
         dpool = ctx.enter_context(tc.tile_pool(name="dpool", bufs=2))
         opool = ctx.enter_context(tc.tile_pool(name="opool", bufs=2))
         psum = ctx.enter_context(tc.psum_pool(name="psum", bufs=8))
@@ -42,13 +46,14 @@ def tile_optimizedlinear_kernel(
         g_v = prev_grad.rearrange("(t p) k -> p t k", p=P)
 
         units = [("x", x_v, 0, 2), ("x", x_v, 2, 2)]
-        units += [("w", w_v, 0, 2), ("w", w_v, 2, 2), ("g", g_v, 0, 4)]
+        units += [("w", w_v, 0, 2), ("w", w_v, 2, 2), ("g", g_v, 0, 2), ("g", g_v, 2, 2)]
         for ch in range(1, O // CHUNK):
             units += [("w", w_v, 4 * ch, 4), ("g", g_v, 4 * ch, 4)]
         n_units = len(units)
 
         raws = {}
         pending = []
+        live = []
         for i in range(n_units):
             for h in range(units[i][3] // 2):
                 pending.append((i, h))
@@ -57,6 +62,8 @@ def tile_optimizedlinear_kernel(
             if len(pending) == 0:
                 return
             i, h = pending[0]
+            if (i, h) == SPREAD_BEFORE:
+                spread_biases()
             pending.remove((i, h))
             kind, view, t0, n = units[i]
             raw = rawp.tile([P, 2, K], BF16, name="raw%d_%d" % (i, h), tag="raw")
@@ -66,6 +73,7 @@ def tile_optimizedlinear_kernel(
             else:
                 nc.sync.dma_start(out=raw[:], in_=view[:, t0 + 2 * h : t0 + 2 * h + 2, :])
             raws[(i, h)] = raw
+            live.append((i, h))
 
         load_next()
         load_next()
@@ -75,17 +83,25 @@ def tile_optimizedlinear_kernel(
         left = consts.tile([P, B], BF16)
         nc.gpsimd.memset(left[:].bitcast(F32), 0.0)
         nc.gpsimd.memset(left[0:1, :], -1.0)
-        right = consts.tile([P, O], BF16)
+        right = consts.tile([P, ND * CHUNK], BF16)
         nc.vector.memset(right[:].bitcast(F32), 0.0)
         ident_bf = consts.tile([P, P], BF16)
         masks.make_identity(nc, ident_bf[:])
         nc.sync.dma_start(out=left[1:2, :], in_=lr_samples.rearrange("(r n) -> r n", n=B))
-        nc.sync.dma_start(out=right[0:1, :], in_=bias.rearrange("(r n) -> r n", n=O))
-        nc.sync.dma_start(out=right[1:2, :], in_=prev_bias_grad.rearrange("(r n) -> r n", n=O))
+        nc.sync.dma_start(out=right[0:1, :], in_=bias[0 : ND * CHUNK].rearrange("(r n) -> r n", n=ND * CHUNK))
+        nc.sync.dma_start(out=right[1:2, :], in_=prev_bias_grad[0 : ND * CHUNK].rearrange("(r n) -> r n", n=ND * CHUNK))
+        neg_lr = consts.tile([P, NBT], F32)
+        lr_col = consts.tile([P, NBT], F32)
+        bias_b = consts.tile([P, O - ND * CHUNK], BF16)
+        pbias_b = consts.tile([P, O - ND * CHUNK], BF16)
+        d_tiles = {}
+
+        def spread_biases():
+            nc.sync.dma_start(out=bias_b[:], in_=bias[ND * CHUNK : O].partition_broadcast(P))
+            nc.sync.dma_start(out=pbias_b[:], in_=prev_bias_grad[ND * CHUNK : O].partition_broadcast(P))
+
         for i in range(2, RAW_BUFS):
             load_next()
-        neg_lr = consts.tile([P, NBT], F32)
-        d_tiles = {}
 
         def copy(eng, dst, src):
             if eng == "S":
@@ -93,33 +109,55 @@ def tile_optimizedlinear_kernel(
             else:
                 nc.vector.tensor_copy(out=dst, in_=src)
 
-        def d_job(ch, bt, eng):
-            bank = psum.tile([P, 512], F32, name="d%d_%d" % (ch, bt), tag="ps")
-            cols = slice(ch * CHUNK, (ch + 1) * CHUNK)
-            nc.tensor.matmul(
-                out=bank[:], lhsT=left[:, bt * P : (bt + 1) * P], rhs=right[:, cols], start=True, stop=True
-            )
+        def d_tile(ch):
             if ch not in d_tiles:
                 d_tiles[ch] = dpool.tile([P, NBT, CHUNK], F32, name="dt%d" % ch, tag="d")
-            copy(eng, d_tiles[ch][:, bt, :], bank[:])
+            return d_tiles[ch]
+
+        def d_job(ch, bt):
+            if ch < ND:
+                cols = slice(ch * CHUNK, (ch + 1) * CHUNK)
+                bank = psum.tile([P, 512], F32, name="d%d_%d" % (ch, bt), tag="ps")
+                nc.tensor.matmul(
+                    out=bank[:], lhsT=left[:, bt * P : (bt + 1) * P], rhs=right[:, cols], start=True, stop=True
+                )
+                copy("S", d_tile(ch)[:, bt, :], bank[:])
+                return
+            cols = slice((ch - ND) * CHUNK, (ch - ND + 1) * CHUNK)
+            nc.vector.scalar_tensor_tensor(
+                out=d_tile(ch)[:, bt, :],
+                in0=pbias_b[:, cols],
+                scalar=lr_col[:, bt : bt + 1],
+                in1=bias_b[:, cols],
+                op0=ALU.mult,
+                op1=ALU.subtract,
+            )
 
         grouped = {}
         codes = {}
         planes = {}
         ordered = {}
 
-        def reorder(i, j0, j1, eng):
-            if i not in ordered:
-                ordered[i] = ordp.tile([P, 4, K // 2], F32, name="ord%d" % i, tag="ord")
-            n = j1 - j0
-            src = raws[(i, j0 // 2)][:, j0 % 2 : j0 % 2 + n, :].bitcast(F32).rearrange("p j (m u) -> p j u m", u=2)
-            dst = ordered[i][:, j0:j1, :].rearrange("p j (u m) -> p j u m", u=2)
-            copy(eng, dst, src)
-            if j1 % 2 == 0:
+        used = {}
+        reordered = set()
+
+        def consumed(i, h):
+            used[(i, h)] = used.get((i, h), 0) + 1
+            while len(live) > 0 and used.get(live[0], 0) == 2:
+                live.remove(live[0])
                 load_next()
 
+        def reorder(i, j, eng):
+            if i not in ordered:
+                ordered[i] = ordp.tile([P, 4, K // 2], F32, name="ord%d" % i, tag="ord")
+            src = raws[(i, j // 2)][:].bitcast(F32)[:, j % 2, :].rearrange("p (m u) -> p u m", u=2)
+            dst = ordered[i][:, j, :].rearrange("p (u m) -> p u m", u=2)
+            copy(eng, dst, src)
+            reordered.add((i, j))
+            consumed(i, j // 2)
+
         def words(i, j, g, u):
-            if i in ordered:
+            if (i, j) in reordered:
                 c0 = 512 * u + P * g
                 return ordered[i][:, j, c0 : c0 + P]
             c0 = 256 * g + u
@@ -140,7 +178,7 @@ def tile_optimizedlinear_kernel(
 
         def x_tile(t):
             i, j = t // 2, t % 2
-            grp = grpp.tile([P, PASSES, 4 * P], BF16, name="xgrp%d" % t, tag="xgrp", align_bytes=64)
+            grp = grpp.tile([P, PASSES, 4 * P], BF16, name="xgrp%d" % t, tag="xgrp", bufs=3, align_bytes=64)
             row_tile_transposes(i, j, grp[:].bitcast(F32), "SS")
             cod = consts.tile([P, PASSES, P], U32, name="xcod%d" % t, align_bytes=256)
             pla = consts.tile([P, PASSES, P], U8, name="xpla%d" % t, align_bytes=256)
@@ -216,7 +254,7 @@ def tile_optimizedlinear_kernel(
             o_sl = o_tiles[ch][:, bt, lo : lo + width]
             if kind == "w":
                 nc.vector.tensor_tensor(
-                    out=o_sl, in0=acc[:, 0:width], in1=d_tiles[ch][:, bt, lo : lo + width], op=ALU.subtract
+                    out=o_sl, in0=acc[:, 0:width], in1=d_tile(ch)[:, bt, lo : lo + width], op=ALU.subtract
                 )
             else:
                 nc.vector.scalar_tensor_tensor(
@@ -229,16 +267,17 @@ def tile_optimizedlinear_kernel(
                 )
                 nc.sync.dma_start(out=out[bt * P : (bt + 1) * P, col : col + width], in_=o_sl)
 
-        x_tile(0)
-        x_tile(1)
-        x_quantise(0)
-        x_tile(2)
-        x_quantise(1)
-        load_next()
-        x_tile(3)
-        x_quantise(2)
-        load_next()
+        def x_all(t):
+            x_tile(t)
+            consumed(t // 2, 0)
 
+        x_all(0)
+        x_all(1)
+        x_quantise(0)
+        x_all(2)
+        x_quantise(1)
+        x_all(3)
+        x_quantise(2)
         lr_ps = psum.tile([P, 512], F32, name="lr_ps", tag="ps")
         for bt in range(NBT):
             nc.tensor.matmul(
@@ -248,53 +287,56 @@ def tile_optimizedlinear_kernel(
                 start=True,
                 stop=True,
             )
-        d_job(0, 0, "S")
-        d_job(0, 1, "S")
 
-        def w_tile(i, j, engines):
+        def w_tile(i, j):
             if j == 0:
                 make_grouped(i)
-            reorder(i, j, j + 1, "V")
-            row_tile_transposes(i, j, grouped[i][:].bitcast(F32)[:, :, 256 * j : 256 * j + 256], engines)
+            row_tile_transposes(i, j, grouped[i][:].bitcast(F32)[:, :, 256 * j : 256 * j + 256], "SS")
+            consumed(i, 0)
 
-        w_tile(2, 0, "SS")
+        w_tile(2, 0)
         nc.vector.tensor_scalar_mul(out=neg_lr[:], in0=lr_ps[:, 0:NBT], scalar1=-1.0)
+        nc.vector.tensor_copy(out=lr_col[:], in_=lr_ps[:, 0:NBT])
         x_quantise(3)
-        w_tile(2, 1, "SS")
-        w_tile(3, 0, "SS")
-        w_tile(3, 1, "SS")
+        w_tile(2, 1)
         quantise(2, 0)
         quantise(2, 2)
-        d_job(0, 2, "S")
-        d_job(0, 3, "S")
+        w_tile(3, 0)
+        w_tile(3, 1)
+        for bt in range(NBT):
+            d_job(0, bt)
 
-        extra = {}
+        d_jobs = {}
         for i in range(2, n_units):
             kind, view, t0, n = units[i]
             ch = (t0 * P) // CHUNK
-            if ch + 1 >= O // CHUNK:
-                extra[i] = []
-            elif n == 2:
-                extra[i] = [(ch + 1, t0 // 2)]
-            else:
-                extra[i] = [(ch + 1, 0), (ch + 1, 1)] if kind == "w" else [(ch + 1, 2), (ch + 1, 3)]
+            d_jobs[i] = []
+            if ch + 1 < O // CHUNK:
+                if n == 4:
+                    d_jobs[i] = [(ch + 1, 0), (ch + 1, 1)] if kind == "w" else [(ch + 1, 2), (ch + 1, 3)]
+                elif kind == "g":
+                    d_jobs[i] = [(ch + 1, t0), (ch + 1, t0 + 1)]
 
         for i in range(2, n_units):
             nxt = i + 1
             far = i + 2
-            n_far = units[far][3] if far < n_units else 0
-            if n_far > 0:
-                if far < 6:
-                    reorder(far, 0, 2, "V")
-                else:
-                    reorder(far, 1, 2, "V")
-                reorder(far, 2, 4, "V")
+            if far < n_units:
+                for j in range(units[far][3]):
+                    if REORDER[far][j] == "V":
+                        reorder(far, j, "V")
+            for ch, bt in d_jobs[i]:
+                if ch >= ND:
+                    d_job(ch, bt)
             if nxt < n_units:
                 if nxt > 3:
                     transposes(nxt, "S")
+                    for j in range(units[nxt][3]):
+                        if REORDER[nxt][j] == "T":
+                            consumed(nxt, j // 2)
                 quantise(nxt, 0)
-            for ch, bt in extra[i]:
-                d_job(ch, bt, "S")
+            for ch, bt in d_jobs[i]:
+                if ch < ND:
+                    d_job(ch, bt)
             if nxt == n_units:
                 for bt in range(NBT):
                     mx_group(i, bt, 0, 256)
@@ -304,6 +346,8 @@ def tile_optimizedlinear_kernel(
             mx_group(i, 1)
             quantise(nxt, 2)
             mx_group(i, 2)
-            if i + 3 >= 6 and i + 3 < n_units:
-                reorder(i + 3, 0, 1, "S")
+            if 6 <= i + 3 < n_units:
+                for j in range(units[i + 3][3]):
+                    if REORDER[i + 3][j] == "S":
+                        reorder(i + 3, j, "S")
             mx_group(i, 3)

@@ -23,7 +23,7 @@ RAW_BUFS = 8
 ND = 2
 SPREAD_BEFORE = (9, 0)
 
-REORDER = {4: "VV", 5: "VV", 6: "SVVV", 7: "TTVV", 8: "SVVV", 9: "SSVV", 10: "SSVV", 11: "SSVV"}
+REORDER = {4: "VV", 5: "VV", 6: "SVVV", 7: "TVVV", 8: "SVVV", 9: "SSVV", 10: "SSVV", 11: "SSVV"}
 
 
 def tile_optimizedlinear_kernel(
@@ -69,7 +69,9 @@ def tile_optimizedlinear_kernel(
             raw = rawp.tile([P, 2, K], BF16, name="raw%d_%d" % (i, h), tag="raw")
             if i < 4:
                 for j in range(2):
-                    nc.sync.dma_start(out=raw[:, j, :], in_=view[:, t0 + 2 * h + j, :])
+                    for k0 in range(0, K, K // 2):
+                        cols = slice(k0, k0 + K // 2)
+                        nc.sync.dma_start(out=raw[:, j, cols], in_=view[:, t0 + 2 * h + j, cols])
             else:
                 nc.sync.dma_start(out=raw[:], in_=view[:, t0 + 2 * h : t0 + 2 * h + 2, :])
             raws[(i, h)] = raw
@@ -114,14 +116,25 @@ def tile_optimizedlinear_kernel(
                 d_tiles[ch] = dpool.tile([P, NBT, CHUNK], F32, name="dt%d" % ch, tag="d")
             return d_tiles[ch]
 
+        d_banks = {}
+
+        def d_matmul(ch, bt):
+            d_banks[bt] = psum.tile([P, 512], F32, name="d%d_%d" % (ch, bt), tag="ps")
+            nc.tensor.matmul(
+                out=d_banks[bt][:],
+                lhsT=left[:, bt * P : (bt + 1) * P],
+                rhs=right[:, ch * CHUNK : (ch + 1) * CHUNK],
+                start=True,
+                stop=True,
+            )
+
+        def d_copy(ch, bt):
+            copy("S", d_tile(ch)[:, bt, :], d_banks[bt][:])
+
         def d_job(ch, bt):
             if ch < ND:
-                cols = slice(ch * CHUNK, (ch + 1) * CHUNK)
-                bank = psum.tile([P, 512], F32, name="d%d_%d" % (ch, bt), tag="ps")
-                nc.tensor.matmul(
-                    out=bank[:], lhsT=left[:, bt * P : (bt + 1) * P], rhs=right[:, cols], start=True, stop=True
-                )
-                copy("S", d_tile(ch)[:, bt, :], bank[:])
+                d_matmul(ch, bt)
+                d_copy(ch, bt)
                 return
             cols = slice((ch - ND) * CHUNK, (ch - ND + 1) * CHUNK)
             nc.vector.scalar_tensor_tensor(
@@ -288,6 +301,9 @@ def tile_optimizedlinear_kernel(
                 stop=True,
             )
 
+        d_matmul(0, 0)
+        d_matmul(0, 1)
+
         def w_tile(i, j):
             if j == 0:
                 make_grouped(i)
@@ -303,8 +319,10 @@ def tile_optimizedlinear_kernel(
         quantise(2, 2)
         w_tile(3, 0)
         w_tile(3, 1)
+        d_matmul(0, 2)
+        d_matmul(0, 3)
         for bt in range(NBT):
-            d_job(0, bt)
+            d_copy(0, bt)
 
         d_jobs = {}
         for i in range(2, n_units):
@@ -324,9 +342,6 @@ def tile_optimizedlinear_kernel(
                 for j in range(units[far][3]):
                     if REORDER[far][j] == "V":
                         reorder(far, j, "V")
-            for ch, bt in d_jobs[i]:
-                if ch >= ND:
-                    d_job(ch, bt)
             if nxt < n_units:
                 if nxt > 3:
                     transposes(nxt, "S")
@@ -340,7 +355,10 @@ def tile_optimizedlinear_kernel(
             if nxt == n_units:
                 for bt in range(NBT):
                     mx_group(i, bt, 0, 256)
-                    mx_group(i, bt, 256, 256)
+                    if bt < NBT - 1:
+                        mx_group(i, bt, 256, 256)
+                mx_group(i, NBT - 1, 256, 128)
+                mx_group(i, NBT - 1, 384, 128)
                 break
             mx_group(i, 0)
             mx_group(i, 1)
@@ -351,3 +369,6 @@ def tile_optimizedlinear_kernel(
                     if REORDER[i + 3][j] == "S":
                         reorder(i + 3, j, "S")
             mx_group(i, 3)
+            for ch, bt in d_jobs[i]:
+                if ch >= ND:
+                    d_job(ch, bt)

from contextlib import ExitStack

import concourse.masks as masks
import concourse.mybir as mybir

F32 = mybir.dt.float32
BF16 = mybir.dt.bfloat16
U32 = mybir.dt.uint32
U8 = mybir.dt.uint8
FP8X4 = mybir.dt.float8_e4m3fn_x4
ALU = mybir.AluOpType

P = 128
B = 512
K = 2048
O = 2048
PASSES = K // 512
NBT = B // P
CHUNK = 512
FLOPS = 2 * 2 * B * K * O

RAW_BUFS = 8
ND = 2
SPREAD_BEFORE = (9, 0)

REORDER = {4: "VV", 5: "VV", 6: "SVVV", 7: "TVVV", 8: "SVVV", 9: "SSVV", 10: "SSVV", 11: "SSVV"}


def tile_optimizedlinear_kernel(
    tc, input_data, weight, bias, prev_grad, prev_bias_grad, lr_samples, out
):
    nc = tc.nc
    with ExitStack() as ctx:
        consts = ctx.enter_context(tc.tile_pool(name="consts", bufs=1))
        rawp = ctx.enter_context(tc.tile_pool(name="rawp", bufs=RAW_BUFS))
        ordp = ctx.enter_context(tc.tile_pool(name="ordp", bufs=3))
        grpp = ctx.enter_context(tc.tile_pool(name="grpp", bufs=2))
        codp = ctx.enter_context(tc.tile_pool(name="codp", bufs=2))
        dpool = ctx.enter_context(tc.tile_pool(name="dpool", bufs=2))
        opool = ctx.enter_context(tc.tile_pool(name="opool", bufs=2))
        psum = ctx.enter_context(tc.psum_pool(name="psum", bufs=8))
        ctx.enter_context(tc.manual_schedule())

        x_v = input_data.rearrange("(t p) k -> p t k", p=P)
        w_v = weight.rearrange("(t p) k -> p t k", p=P)
        g_v = prev_grad.rearrange("(t p) k -> p t k", p=P)

        units = [("x", x_v, 0, 2), ("x", x_v, 2, 2)]
        units += [("w", w_v, 0, 2), ("w", w_v, 2, 2), ("g", g_v, 0, 2), ("g", g_v, 2, 2)]
        for ch in range(1, O // CHUNK):
            units += [("w", w_v, 4 * ch, 4), ("g", g_v, 4 * ch, 4)]
        n_units = len(units)

        raws = {}
        pending = []
        live = []
        for i in range(n_units):
            for h in range(units[i][3] // 2):
                pending.append((i, h))

        def load_next():
            if len(pending) == 0:
                return
            i, h = pending[0]
            if (i, h) == SPREAD_BEFORE:
                spread_biases()
            pending.remove((i, h))
            kind, view, t0, n = units[i]
            raw = rawp.tile([P, 2, K], BF16, name="raw%d_%d" % (i, h), tag="raw")
            if i < 4:
                for j in range(2):
                    for k0 in range(0, K, K // 2):
                        cols = slice(k0, k0 + K // 2)
                        nc.sync.dma_start(out=raw[:, j, cols], in_=view[:, t0 + 2 * h + j, cols])
            else:
                nc.sync.dma_start(out=raw[:], in_=view[:, t0 + 2 * h : t0 + 2 * h + 2, :])
            raws[(i, h)] = raw
            live.append((i, h))

        load_next()
        load_next()

        ident = consts.tile([P, P], F32)
        masks.make_identity(nc, ident[:])
        left = consts.tile([P, B], BF16)
        nc.gpsimd.memset(left[:].bitcast(F32), 0.0)
        nc.gpsimd.memset(left[0:1, :], -1.0)
        right = consts.tile([P, ND * CHUNK], BF16)
        nc.vector.memset(right[:].bitcast(F32), 0.0)
        ident_bf = consts.tile([P, P], BF16)
        masks.make_identity(nc, ident_bf[:])
        nc.sync.dma_start(out=left[1:2, :], in_=lr_samples.rearrange("(r n) -> r n", n=B))
        nc.sync.dma_start(out=right[0:1, :], in_=bias[0 : ND * CHUNK].rearrange("(r n) -> r n", n=ND * CHUNK))
        nc.sync.dma_start(out=right[1:2, :], in_=prev_bias_grad[0 : ND * CHUNK].rearrange("(r n) -> r n", n=ND * CHUNK))
        neg_lr = consts.tile([P, NBT], F32)
        lr_col = consts.tile([P, NBT], F32)
        bias_b = consts.tile([P, O - ND * CHUNK], BF16)
        pbias_b = consts.tile([P, O - ND * CHUNK], BF16)
        d_tiles = {}

        def spread_biases():
            nc.sync.dma_start(out=bias_b[:], in_=bias[ND * CHUNK : O].partition_broadcast(P))
            nc.sync.dma_start(out=pbias_b[:], in_=prev_bias_grad[ND * CHUNK : O].partition_broadcast(P))

        for i in range(2, RAW_BUFS):
            load_next()

        def copy(eng, dst, src):
            if eng == "S":
                nc.scalar.copy(out=dst, in_=src)
            else:
                nc.vector.tensor_copy(out=dst, in_=src)

        def d_tile(ch):
            if ch not in d_tiles:
                d_tiles[ch] = dpool.tile([P, NBT, CHUNK], F32, name="dt%d" % ch, tag="d")
            return d_tiles[ch]

        d_banks = {}

        def d_matmul(ch, bt):
            d_banks[bt] = psum.tile([P, 512], F32, name="d%d_%d" % (ch, bt), tag="ps")
            nc.tensor.matmul(
                out=d_banks[bt][:],
                lhsT=left[:, bt * P : (bt + 1) * P],
                rhs=right[:, ch * CHUNK : (ch + 1) * CHUNK],
                start=True,
                stop=True,
            )

        def d_copy(ch, bt):
            copy("S", d_tile(ch)[:, bt, :], d_banks[bt][:])

        def d_job(ch, bt):
            if ch < ND:
                d_matmul(ch, bt)
                d_copy(ch, bt)
                return
            cols = slice((ch - ND) * CHUNK, (ch - ND + 1) * CHUNK)
            nc.vector.scalar_tensor_tensor(
                out=d_tile(ch)[:, bt, :],
                in0=pbias_b[:, cols],
                scalar=lr_col[:, bt : bt + 1],
                in1=bias_b[:, cols],
                op0=ALU.mult,
                op1=ALU.subtract,
            )

        grouped = {}
        codes = {}
        planes = {}
        ordered = {}

        used = {}
        reordered = set()

        def consumed(i, h):
            used[(i, h)] = used.get((i, h), 0) + 1
            while len(live) > 0 and used.get(live[0], 0) == 2:
                live.remove(live[0])
                load_next()

        def reorder(i, j, eng):
            if i not in ordered:
                ordered[i] = ordp.tile([P, 4, K // 2], F32, name="ord%d" % i, tag="ord")
            src = raws[(i, j // 2)][:].bitcast(F32)[:, j % 2, :].rearrange("p (m u) -> p u m", u=2)
            dst = ordered[i][:, j, :].rearrange("p (u m) -> p u m", u=2)
            copy(eng, dst, src)
            reordered.add((i, j))
            consumed(i, j // 2)

        def words(i, j, g, u):
            if (i, j) in reordered:
                c0 = 512 * u + P * g
                return ordered[i][:, j, c0 : c0 + P]
            c0 = 256 * g + u
            return raws[(i, j // 2)][:].bitcast(F32)[:, j % 2, c0 : c0 + 255 : 2]

        def row_tile_transposes(i, j, grp_w, engines):
            for half in range(2):
                bank = psum.tile([P, 512], F32, name="bank%d_%d_%d" % (i, j, half), tag="ps")
                for gi in range(2):
                    for u in range(2):
                        s = 2 * gi + u
                        nc.tensor.transpose(bank[:, s * P : (s + 1) * P], words(i, j, 2 * half + gi, u), ident[:])
                copy(
                    engines[half],
                    grp_w[:, 2 * half : 2 * half + 2, :].rearrange("p g (o u) -> p g o u", u=2),
                    bank[:].rearrange("p (g u o) -> p g o u", g=2, u=2),
                )

        def x_tile(t):
            i, j = t // 2, t % 2
            grp = grpp.tile([P, PASSES, 4 * P], BF16, name="xgrp%d" % t, tag="xgrp", bufs=3, align_bytes=64)
            row_tile_transposes(i, j, grp[:].bitcast(F32), "SS")
            cod = consts.tile([P, PASSES, P], U32, name="xcod%d" % t, align_bytes=256)
            pla = consts.tile([P, PASSES, P], U8, name="xpla%d" % t, align_bytes=256)
            codes[("x", t)] = cod
            planes[("x", t)] = pla
            grouped[("x", t)] = grp

        def x_quantise(t):
            nc.vector.quantize_mx(
                out=codes[("x", t)][:].rearrange("p g n -> p (g n)").bitcast(FP8X4),
                scales=planes[("x", t)][:].rearrange("p g n -> p (g n)"),
                in_=grouped[("x", t)][:].rearrange("p g c -> p (g c)"),
            )

        def make_grouped(i):
            width = units[i][3] * P
            grouped[i] = grpp.tile([P, PASSES, 4 * width], BF16, name="grp%d" % i, tag="grp", align_bytes=64)

        def transposes(i, pattern):
            n = units[i][3]
            make_grouped(i)
            grp_w = grouped[i][:].bitcast(F32)
            b = 0
            for g in range(PASSES):
                for h in range(n // 2):
                    bank = psum.tile([P, 512], F32, name="bank%d_%d" % (i, b), tag="ps")
                    for j in range(2):
                        for u in range(2):
                            s = 2 * j + u
                            nc.tensor.transpose(
                                bank[:, s * P : (s + 1) * P], words(i, 2 * h + j, g, u), ident[:]
                            )
                    copy(
                        pattern[b % len(pattern)],
                        grp_w[:, g, 512 * h : 512 * h + 512].rearrange("p (j o u) -> p j o u", j=2, u=2),
                        bank[:].rearrange("p (j u o) -> p j o u", j=2, u=2),
                    )
                    b += 1

        def quantise(i, g0):
            width = units[i][3] * P
            if g0 == 0:
                codes[i] = codp.tile([P, PASSES, width], U32, name="cod%d" % i, tag="cod", align_bytes=256)
                planes[i] = codp.tile([P, PASSES, width], U8, name="pla%d" % i, tag="pla", align_bytes=256)
            nc.vector.quantize_mx(
                out=codes[i][:, g0 : g0 + 2, :].rearrange("p g n -> p (g n)").bitcast(FP8X4),
                scales=planes[i][:, g0 : g0 + 2, :].rearrange("p g n -> p (g n)"),
                in_=grouped[i][:, g0 : g0 + 2, :].rearrange("p g c -> p (g c)"),
            )

        o_tiles = {}

        def mx_group(i, bt, first=0, width=None):
            kind, view, t0, n = units[i]
            if width is None:
                width = n * P
            acc = psum.tile([P, 512], F32, name="acc%d_%d_%d" % (i, bt, first), tag="ps")
            for g in range(PASSES):
                nc.tensor.matmul_mx(
                    out=acc[:, 0:width],
                    lhsT=codes[("x", bt)][:, g, :].bitcast(FP8X4),
                    lhsT_scale=planes[("x", bt)][:, g, :],
                    rhs=codes[i][:, g, first : first + width].bitcast(FP8X4),
                    rhs_scale=planes[i][:, g, first : first + width],
                    start=(g == 0),
                    stop=(g == PASSES - 1),
                )
            ch = (t0 * P) // CHUNK
            col = t0 * P + first
            lo = col - ch * CHUNK
            if ch not in o_tiles:
                o_tiles[ch] = opool.tile([P, NBT, CHUNK], F32, name="o%d" % ch, tag="o")
            o_sl = o_tiles[ch][:, bt, lo : lo + width]
            if kind == "w":
                nc.vector.tensor_tensor(
                    out=o_sl, in0=acc[:, 0:width], in1=d_tile(ch)[:, bt, lo : lo + width], op=ALU.subtract
                )
            else:
                nc.vector.scalar_tensor_tensor(
                    out=o_sl,
                    in0=acc[:, 0:width],
                    scalar=neg_lr[:, bt : bt + 1],
                    in1=o_sl,
                    op0=ALU.mult,
                    op1=ALU.add,
                )
                nc.sync.dma_start(out=out[bt * P : (bt + 1) * P, col : col + width], in_=o_sl)

        def x_all(t):
            x_tile(t)
            consumed(t // 2, 0)

        x_all(0)
        x_all(1)
        x_quantise(0)
        x_all(2)
        x_quantise(1)
        x_all(3)
        x_quantise(2)
        lr_ps = psum.tile([P, 512], F32, name="lr_ps", tag="ps")
        for bt in range(NBT):
            nc.tensor.matmul(
                out=lr_ps[:, bt : bt + 1],
                lhsT=left[:, bt * P : (bt + 1) * P],
                rhs=ident_bf[:, 1:2],
                start=True,
                stop=True,
            )

        d_matmul(0, 0)
        d_matmul(0, 1)

        def w_tile(i, j):
            if j == 0:
                make_grouped(i)
            row_tile_transposes(i, j, grouped[i][:].bitcast(F32)[:, :, 256 * j : 256 * j + 256], "SS")
            consumed(i, 0)

        w_tile(2, 0)
        nc.vector.tensor_scalar_mul(out=neg_lr[:], in0=lr_ps[:, 0:NBT], scalar1=-1.0)
        nc.vector.tensor_copy(out=lr_col[:], in_=lr_ps[:, 0:NBT])
        x_quantise(3)
        w_tile(2, 1)
        quantise(2, 0)
        quantise(2, 2)
        w_tile(3, 0)
        w_tile(3, 1)
        d_matmul(0, 2)
        d_matmul(0, 3)
        for bt in range(NBT):
            d_copy(0, bt)

        d_jobs = {}
        for i in range(2, n_units):
            kind, view, t0, n = units[i]
            ch = (t0 * P) // CHUNK
            d_jobs[i] = []
            if ch + 1 < O // CHUNK:
                if n == 4:
                    d_jobs[i] = [(ch + 1, 0), (ch + 1, 1)] if kind == "w" else [(ch + 1, 2), (ch + 1, 3)]
                elif kind == "g":
                    d_jobs[i] = [(ch + 1, t0), (ch + 1, t0 + 1)]

        for i in range(2, n_units):
            nxt = i + 1
            far = i + 2
            if far < n_units:
                for j in range(units[far][3]):
                    if REORDER[far][j] == "V":
                        reorder(far, j, "V")
            if nxt < n_units:
                if nxt > 3:
                    transposes(nxt, "S")
                    for j in range(units[nxt][3]):
                        if REORDER[nxt][j] == "T":
                            consumed(nxt, j // 2)
                quantise(nxt, 0)
            for ch, bt in d_jobs[i]:
                if ch < ND:
                    d_job(ch, bt)
            if nxt == n_units:
                for bt in range(NBT):
                    mx_group(i, bt, 0, 256)
                    if bt < NBT - 1:
                        mx_group(i, bt, 256, 256)
                mx_group(i, NBT - 1, 256, 128)
                mx_group(i, NBT - 1, 384, 128)
                break
            mx_group(i, 0)
            mx_group(i, 1)
            quantise(nxt, 2)
            mx_group(i, 2)
            if 6 <= i + 3 < n_units:
                for j in range(units[i + 3][3]):
                    if REORDER[i + 3][j] == "S":
                        reorder(i + 3, j, "S")
            mx_group(i, 3)
            for ch, bt in d_jobs[i]:
                if ch >= ND:
                    d_job(ch, bt)
